import numpy as np
import ml_dtypes


def mxq(x, axis, fmt="e4m3"):
    dtype, down = {"e4m3": (ml_dtypes.float8_e4m3fn, 7), "e5m2": (ml_dtypes.float8_e5m2, 14)}[fmt]
    v = np.moveaxis(np.asarray(x, np.float32).astype(ml_dtypes.bfloat16).astype(np.float64), axis, -1)
    blocks = v.reshape(v.shape[:-1] + (-1, 32))
    amax = np.abs(blocks).max(-1, keepdims=True)
    byte = np.maximum(np.where(amax > 0, np.frexp(amax)[1] - 1 + 127, 0) - down, 1)
    scale = np.exp2(byte - 127.0)
    codes = (blocks / scale).astype(np.float32).astype(dtype).astype(np.float64)
    return np.moveaxis((codes * scale).reshape(v.shape), -1, axis)


WIDE = False


def mx_kscale(k):
    if not WIDE:
        return np.ones(k)
    levels = np.array([10, -10, 5, -5, 0])
    a = np.random.permutation(np.resize(levels, k // 512 * 4)).reshape(k // 512, 4)
    idx = np.arange(k)
    return np.exp2(a[idx // 512, idx % 128 // 32])


BF16 = ml_dtypes.bfloat16


def bf(x):
    return np.asarray(x, np.float32).astype(BF16)


def f64(x):
    return np.asarray(x).astype(np.float64)


B, S, D, E, F = 4, 1024, 1024, 256, 4096
EPS = 1e-5


def layernorm(x, g, b):
    m = x.mean(-1, keepdims=True)
    v = ((x - m) ** 2).mean(-1, keepdims=True)
    return (x - m) * (1.0 / np.sqrt(v + EPS)) * g + b


def rotate_half(x):
    return np.concatenate([-x[..., ::2], x[..., 1::2]], axis=-1)


def sinu_pos_emb(dim, length):
    inv_freq = 1.0 / 10000.0 ** (np.arange(0, dim, 2) / dim)
    sp = np.arange(length)[:, None] * inv_freq[None, :]
    return np.concatenate([np.sin(sp), np.cos(sp)], axis=-1)


def setup_inputs():
    s = mx_kscale(D)
    return {"src": bf(np.random.standard_normal((B, S, D)) + 0.5),
            "Wqkv": bf(np.random.standard_normal((3 * E, D)) / np.sqrt(D) / s[None, :]),
            "bqkv": bf(0.1 * np.random.standard_normal(3 * E)),
            "g1": bf((1.0 + 0.1 * np.random.standard_normal(D)) * s),
            "be1": bf(0.1 * np.random.standard_normal(D) * s)}


def reference(src, Wqkv, bqkv, g1, be1):
    xn = layernorm(f64(src), f64(g1), f64(be1))
    qkv = (mxq(xn, 2, "e4m3") @ mxq(f64(Wqkv), 1, "e4m3").T) + f64(bqkv)
    Q, K, V = qkv[..., :E], qkv[..., E:2 * E], qkv[..., 2 * E:]
    emb = sinu_pos_emb(E, S)
    c, s = np.cos(emb), np.sin(emb)
    Q = Q * c + rotate_half(Q) * s
    K = K * c - rotate_half(K) * s
    return Q, K, V

@@ -1,0 +1,260 @@
+import math
+
+import concourse.mybir as mybir
+from concourse.masks import make_identity
+
+F32 = mybir.dt.float32
+BF16 = mybir.dt.bfloat16
+I32 = mybir.dt.int32
+U32 = mybir.dt.uint32
+U8 = mybir.dt.uint8
+FP8X4 = mybir.dt.float8_e4m3fn_x4
+ALU = mybir.AluOpType
+ACT = mybir.ActivationFunctionType
+
+P = 128
+BATCH = 4
+SEQ = 1024
+D = 1024
+E = 256
+HALF = E // 2
+N_OUT = 3 * E
+EPS = 1e-5
+
+PACK = 4
+K_PASS = P * PACK
+PASSES = D // K_PASS
+CHUNKS = D // P
+POS_TILES = SEQ // P
+TOKENS = BATCH * P
+BN_CHUNK = 512
+
+FREQ_RATIO = 10000.0 ** (-1.0 / HALF)
+ROUND_MAGIC = 12582912.0
+TWO_PI_HI = 6.28125
+TWO_PI_LO = 2.0 * math.pi - TWO_PI_HI
+
+FLOPS = 2 * BATCH * SEQ * D * N_OUT
+
+
+def build_position_tables(nc, work, cos_tab, sin_tab):
+    freq = work.tile([P, HALF], F32)
+    nc.vector.memset(freq[:, 0:1], 1.0)
+    for doubling in range(7):
+        n = 2**doubling
+        nc.vector.tensor_scalar(
+            out=freq[:, n : 2 * n], in0=freq[:, 0:n], scalar1=FREQ_RATIO**n, scalar2=None, op0=ALU.mult
+        )
+    pos_int = work.tile([P, POS_TILES], I32)
+    nc.gpsimd.iota(pos_int[:], pattern=[[P, POS_TILES]], base=0, channel_multiplier=1)
+    pos = work.tile([P, POS_TILES], F32)
+    nc.vector.tensor_copy(out=pos[:], in_=pos_int[:])
+
+    shape = [P, POS_TILES, HALF]
+    angle = work.tile(shape, F32)
+    nc.vector.tensor_tensor(
+        out=angle[:],
+        in0=freq[:].unsqueeze(1).to_broadcast(shape),
+        in1=pos[:].unsqueeze(2).to_broadcast(shape),
+        op=ALU.mult,
+    )
+    turns = work.tile(shape, F32)
+    nc.vector.tensor_scalar(
+        out=turns[:], in0=angle[:], scalar1=0.5 / math.pi, scalar2=ROUND_MAGIC, op0=ALU.mult, op1=ALU.add
+    )
+    nc.vector.tensor_scalar(out=turns[:], in0=turns[:], scalar1=ROUND_MAGIC, scalar2=None, op0=ALU.subtract)
+    nc.vector.scalar_tensor_tensor(
+        out=angle[:], in0=turns[:], scalar=-TWO_PI_HI, in1=angle[:], op0=ALU.mult, op1=ALU.add
+    )
+    nc.vector.scalar_tensor_tensor(
+        out=angle[:], in0=turns[:], scalar=-TWO_PI_LO, in1=angle[:], op0=ALU.mult, op1=ALU.add
+    )
+    sin_half = work.tile(shape, F32)
+    nc.scalar.activation(out=sin_half[:], in_=angle[:], func=ACT.Sin, scale=0.5)
+    nc.scalar.activation(out=angle[:], in_=angle[:], func=ACT.Abs)
+    nc.vector.tensor_scalar(
+        out=angle[:], in0=angle[:], scalar1=-0.5, scalar2=0.5 * math.pi, op0=ALU.mult, op1=ALU.add
+    )
+    cos_half = work.tile(shape, F32)
+    nc.scalar.activation(out=cos_half[:], in_=angle[:], func=ACT.Sin)
+    emb = work.tile([P, POS_TILES, E], F32)
+    nc.vector.scalar_tensor_tensor(
+        out=emb[:, :, 0:HALF], in0=sin_half[:], scalar=2.0, in1=cos_half[:], op0=ALU.mult, op1=ALU.mult
+    )
+    nc.scalar.activation(out=sin_half[:], in_=sin_half[:], func=ACT.Square)
+    nc.vector.tensor_scalar(
+        out=emb[:, :, HALF:E], in0=sin_half[:], scalar1=-2.0, scalar2=1.0, op0=ALU.mult, op1=ALU.add
+    )
+    nc.scalar.activation(out=sin_tab[:, :, 0:HALF], in_=emb[:, :, 0:HALF], func=ACT.Sin, scale=-1.0)
+    nc.scalar.activation(out=sin_tab[:, :, HALF:E], in_=emb[:, :, HALF:E], func=ACT.Sin)
+    nc.vector.tensor_scalar(out=emb[:], in0=emb[:], scalar1=0.5 * math.pi, scalar2=None, op0=ALU.add)
+    nc.scalar.activation(out=cos_tab[:], in_=emb[:], func=ACT.Sin)
+
+
+def tile_rotaryembeddingtransformerlayer_pa_t_kernel(
+    tc, src, Wqkv, bqkv, g1, be1, out_0, out_1, out_2
+):
+    nc = tc.nc
+    with (
+        tc.tile_pool(name="const", bufs=1) as const,
+        tc.tile_pool(name="work", bufs=1) as work,
+        tc.tile_pool(name="xin", bufs=3) as xin,
+        tc.tile_pool(name="small", bufs=3) as small,
+        tc.tile_pool(name="norm", bufs=2) as norm,
+        tc.tile_pool(name="planes", bufs=1) as plane_pool,
+        tc.tile_pool(name="quant", bufs=2) as quant,
+        tc.tile_pool(name="mix", bufs=2) as mix,
+        tc.psum_pool(name="psum_t", bufs=4) as psum_t,
+        tc.psum_pool(name="psum_qk", bufs=2) as psum_qk,
+        tc.psum_pool(name="psum_v", bufs=2) as psum_v,
+    ):
+        ident_f32 = const.tile([P, P], F32)
+        make_identity(nc, ident_f32[:])
+        ident_bf16 = const.tile([P, P], BF16)
+        make_identity(nc, ident_bf16[:])
+        minus_half = const.tile([P, BATCH], F32)
+        nc.vector.memset(minus_half[:], -0.5)
+
+        w_rows = work.tile([P, N_OUT // P, D], BF16)
+        nc.sync.dma_start(out=w_rows[:], in_=Wqkv.rearrange("(r p) k -> p r k", p=P))
+        gain_rows = work.tile([P, P], BF16)
+        nc.vector.memset(gain_rows[:], 0.0)
+        nc.sync.dma_start(out=gain_rows[0:CHUNKS, :], in_=g1.rearrange("(c p) -> c p", p=P))
+        nc.sync.dma_start(out=gain_rows[CHUNKS : 2 * CHUNKS, :], in_=be1.rearrange("(c p) -> c p", p=P))
+        bias_all = const.tile([P, N_OUT], BF16)
+        nc.sync.dma_start(out=bias_all[:], in_=bqkv.partition_broadcast(P))
+
+        gain_ps = psum_t.tile([P, P], BF16, tag="zT")
+        nc.tensor.transpose(gain_ps[:], gain_rows[:], ident_bf16[:])
+        gain = const.tile([P, 2 * CHUNKS], F32)
+        nc.vector.tensor_copy(out=gain[:], in_=gain_ps[:, 0 : 2 * CHUNKS])
+
+        w_grouped = work.tile([P, PASSES, N_OUT, PACK], BF16, align_bytes=64)
+        w_codes = const.tile([P, PASSES, N_OUT], U32, align_bytes=64)
+        w_scales = const.tile([P, PASSES, N_OUT], U8, align_bytes=64)
+        for c in range(PASSES):
+            for pair in range(N_OUT // (2 * P)):
+                wT = psum_t.tile([P, PACK, 2 * P], BF16, tag="zT")
+                for j in range(PACK):
+                    for h in range(2):
+                        k0 = (PACK * c + j) * P
+                        nc.tensor.transpose(
+                            wT[:, j, h * P : (h + 1) * P], w_rows[:, 2 * pair + h, k0 : k0 + P], ident_bf16[:]
+                        )
+                nc.vector.tensor_copy(
+                    out=w_grouped[:, c, 2 * P * pair : 2 * P * (pair + 1), :],
+                    in_=wT[:].rearrange("p j n -> p n j"),
+                )
+            for lo, hi in ((0, 2 * E), (2 * E, N_OUT)):
+                nc.vector.quantize_mx(
+                    out=w_codes[:, c, lo:hi].bitcast(FP8X4),
+                    scales=w_scales[:, c, lo:hi],
+                    in_=w_grouped[:, c, lo:hi, :].rearrange("p n j -> p (n j)"),
+                )
+
+        cos_tab = const.tile([P, POS_TILES, E], F32)
+        sin_tab = const.tile([P, POS_TILES, E], F32)
+        build_position_tables(nc, work, cos_tab, sin_tab)
+
+        for t in range(POS_TILES):
+            rows = slice(t * P, (t + 1) * P)
+            x = xin.tile([P, BATCH, D], BF16)
+            nc.sync.dma_start(out=x[:], in_=src[:, rows, :].rearrange("b p k -> p b k"))
+
+            stats = small.tile([P, BATCH, D // BN_CHUNK, 6], F32)
+            mean_var = small.tile([P, BATCH, 2], F32)
+            for b in range(BATCH):
+                for h in range(D // BN_CHUNK):
+                    nc.vector.bn_stats(out=stats[:, b, h, :], in_=x[:, b, h * BN_CHUNK : (h + 1) * BN_CHUNK])
+                nc.vector.bn_aggr(out=mean_var[:, b, :], in_=stats[:, b, :, :].rearrange("p h s -> p (h s)"))
+            var_eps = small.tile([P, BATCH], F32)
+            nc.vector.tensor_scalar(out=var_eps[:], in0=mean_var[:, :, 1], scalar1=EPS, scalar2=None, op0=ALU.add)
+            rstd = small.tile([P, BATCH], F32)
+            nc.gpsimd.tensor_tensor(out=rstd[:], in0=var_eps[:], in1=minus_half[:], op=ALU.pow)
+            shift = small.tile([P, BATCH], F32)
+            nc.vector.scalar_tensor_tensor(
+                out=shift[:], in0=mean_var[:, :, 0], scalar=-1.0, in1=rstd[:], op0=ALU.mult, op1=ALU.mult
+            )
+            z = norm.tile([P, BATCH, D], F32)
+            for b in range(BATCH):
+                nc.scalar.activation(
+                    out=z[:, b, :], in_=x[:, b, :], func=ACT.Identity,
+                    scale=rstd[:, b : b + 1], bias=shift[:, b : b + 1],
+                )
+
+            planes = plane_pool.tile([P, CHUNKS, TOKENS], BF16)
+            for kc in range(CHUNKS):
+                zT = psum_t.tile([P, TOKENS], F32, tag="zT")
+                for b in range(BATCH):
+                    nc.tensor.transpose(zT[:, b * P : (b + 1) * P], z[:, b, kc * P : (kc + 1) * P], ident_f32[:])
+                nc.scalar.activation(
+                    out=planes[:, kc, :], in_=zT[:], func=ACT.Identity,
+                    scale=gain[:, kc : kc + 1], bias=gain[:, CHUNKS + kc : CHUNKS + kc + 1],
+                )
+            grouped = quant.tile([P, PASSES, TOKENS, PACK], BF16, align_bytes=64)
+            codes = quant.tile([P, PASSES, TOKENS], U32, align_bytes=64)
+            scales = quant.tile([P, PASSES, TOKENS], U8, align_bytes=64)
+            for c in range(PASSES):
+                nc.scalar.copy(
+                    out=grouped[:, c, :, :].rearrange("p (m i) j -> p m j i", i=4),
+                    in_=planes[:, PACK * c : PACK * (c + 1), :].rearrange("p j (m i) -> p m j i", i=4),
+                )
+            for c in range(PASSES):
+                nc.vector.quantize_mx(
+                    out=codes[:, c, :].bitcast(FP8X4),
+                    scales=scales[:, c, :],
+                    in_=grouped[:, c, :, :].rearrange("p w j -> p (w j)"),
+                )
+
+            qk = mix.tile([P, BATCH, 2, E], F32)
+            v = mix.tile([P, BATCH, E], F32)
+            for b in range(BATCH):
+                tok = slice(b * P, (b + 1) * P)
+                acc_qk = psum_qk.tile([P, 2 * E], F32)
+                for c in range(PASSES):
+                    nc.tensor.matmul_mx(
+                        out=acc_qk[:],
+                        lhsT=codes[:, c, tok].bitcast(FP8X4), lhsT_scale=scales[:, c, tok],
+                        rhs=w_codes[:, c, 0 : 2 * E].bitcast(FP8X4), rhs_scale=w_scales[:, c, 0 : 2 * E],
+                        start=(c == 0), stop=(c == PASSES - 1),
+                    )
+                nc.vector.tensor_tensor(
+                    out=qk[:, b, :, :].rearrange("p q e -> p (q e)"), in0=acc_qk[:], in1=bias_all[:, 0 : 2 * E],
+                    op=ALU.add,
+                )
+                if b % 2 == 0:
+                    acc_v = psum_v.tile([P, 2, E], F32)
+                for c in range(PASSES):
+                    nc.tensor.matmul_mx(
+                        out=acc_v[:, b % 2, :],
+                        lhsT=codes[:, c, tok].bitcast(FP8X4), lhsT_scale=scales[:, c, tok],
+                        rhs=w_codes[:, c, 2 * E : N_OUT].bitcast(FP8X4), rhs_scale=w_scales[:, c, 2 * E : N_OUT],
+                        start=(c == 0), stop=(c == PASSES - 1),
+                    )
+                if b % 2 == 1:
+                    nc.vector.tensor_tensor(
+                        out=v[:, b - 1 : b + 1, :], in0=acc_v[:],
+                        in1=bias_all[:, 2 * E : N_OUT].unsqueeze(1).to_broadcast([P, 2, E]), op=ALU.add,
+                    )
+            nc.sync.dma_start(out=out_2[:, rows, :].rearrange("b p e -> p b e"), in_=v[:])
+
+            straight = mix.tile([P, BATCH, 2, E], F32)
+            turned = mix.tile([P, BATCH, 2, E], F32)
+            nc.gpsimd.tensor_tensor(
+                out=straight[:].rearrange("p b q e -> p (b q) e"),
+                in0=qk[:].rearrange("p b q e -> p (b q) e"),
+                in1=cos_tab[:, t, :].unsqueeze(1).to_broadcast([P, 2 * BATCH, E]),
+                op=ALU.mult,
+            )
+            nc.gpsimd.tensor_tensor(
+                out=turned[:].rearrange("p b q (h i) -> p (b q) h i", h=2),
+                in0=qk[:].rearrange("p b q (i h) -> p (b q) h i", h=2),
+                in1=sin_tab[:, t, :].rearrange("p (h i) -> p h i", h=2).unsqueeze(1).to_broadcast([P, 2 * BATCH, 2, HALF]),
+                op=ALU.mult,
+            )
+            nc.vector.tensor_tensor(out=straight[:, :, 0, :], in0=straight[:, :, 0, :], in1=turned[:, :, 0, :], op=ALU.add)
+            nc.vector.tensor_tensor(
+                out=straight[:, :, 1, :], in0=straight[:, :, 1, :], in1=turned[:, :, 1, :], op=ALU.subtract
+            )
+            nc.sync.dma_start(out=out_0[:, rows, :].rearrange("b p e -> p b e"), in_=straight[:, :, 0, :])
+            nc.sync.dma_start(out=out_1[:, rows, :].rearrange("b p e -> p b e"), in_=straight[:, :, 1, :])

@@ -25,14 +25,13 @@ PACK = 4
 K_PASS = P * PACK
 PASSES = D // K_PASS
 CHUNKS = D // P
-POS_TILES = SEQ // P
+ROUNDS = SEQ // P
 TOKENS = BATCH * P
 BN_CHUNK = 512
+T_BANKS = 4
 
 FREQ_RATIO = 10000.0 ** (-1.0 / HALF)
 ROUND_MAGIC = 12582912.0
-TWO_PI_HI = 6.28125
-TWO_PI_LO = 2.0 * math.pi - TWO_PI_HI
 
 FLOPS = 2 * BATCH * SEQ * D * N_OUT
 
@@ -40,55 +39,40 @@ FLOPS = 2 * BATCH * SEQ * D * N_OUT
 def build_position_tables(nc, work, cos_tab, sin_tab):
     freq = work.tile([P, HALF], F32)
     nc.vector.memset(freq[:, 0:1], 1.0)
+    nc.vector.tensor_scalar(out=freq[:, 0:1], in0=freq[:, 0:1], scalar1=0.5 / math.pi, scalar2=None, op0=ALU.mult)
     for doubling in range(7):
         n = 2**doubling
         nc.vector.tensor_scalar(
             out=freq[:, n : 2 * n], in0=freq[:, 0:n], scalar1=FREQ_RATIO**n, scalar2=None, op0=ALU.mult
         )
-    pos_int = work.tile([P, POS_TILES], I32)
-    nc.gpsimd.iota(pos_int[:], pattern=[[P, POS_TILES]], base=0, channel_multiplier=1)
-    pos = work.tile([P, POS_TILES], F32)
+    quarter_turn = work.tile([P, 1], F32)
+    nc.vector.memset(quarter_turn[:], 1.0)
+    nc.vector.tensor_scalar(out=quarter_turn[:], in0=quarter_turn[:], scalar1=0.5 * math.pi, scalar2=None, op0=ALU.mult)
+    pos_int = work.tile([P, ROUNDS], I32)
+    nc.gpsimd.iota(pos_int[:], pattern=[[P, ROUNDS]], base=0, channel_multiplier=1)
+    pos = work.tile([P, ROUNDS], F32)
     nc.vector.tensor_copy(out=pos[:], in_=pos_int[:])
 
-    shape = [P, POS_TILES, HALF]
-    angle = work.tile(shape, F32)
+    turns = work.tile([P, ROUNDS, E], F32)
+    half_shape = [P, ROUNDS, HALF]
     nc.vector.tensor_tensor(
-        out=angle[:],
-        in0=freq[:].unsqueeze(1).to_broadcast(shape),
-        in1=pos[:].unsqueeze(2).to_broadcast(shape),
+        out=turns[:, :, 0:HALF],
+        in0=freq[:].unsqueeze(1).to_broadcast(half_shape),
+        in1=pos[:].unsqueeze(2).to_broadcast(half_shape),
         op=ALU.mult,
     )
-    turns = work.tile(shape, F32)
-    nc.vector.tensor_scalar(
-        out=turns[:], in0=angle[:], scalar1=0.5 / math.pi, scalar2=ROUND_MAGIC, op0=ALU.mult, op1=ALU.add
-    )
-    nc.vector.tensor_scalar(out=turns[:], in0=turns[:], scalar1=ROUND_MAGIC, scalar2=None, op0=ALU.subtract)
+    nc.vector.tensor_scalar(out=turns[:, :, HALF:E], in0=turns[:, :, 0:HALF], scalar1=0.25, scalar2=None, op0=ALU.add)
+    whole = work.tile([P, ROUNDS, E], F32)
+    nc.vector.tensor_scalar(out=whole[:], in0=turns[:], scalar1=ROUND_MAGIC, scalar2=None, op0=ALU.add)
+    minus_f = work.tile([P, ROUNDS, E], F32)
     nc.vector.scalar_tensor_tensor(
-        out=angle[:], in0=turns[:], scalar=-TWO_PI_HI, in1=angle[:], op0=ALU.mult, op1=ALU.add
+        out=minus_f[:], in0=whole[:], scalar=ROUND_MAGIC, in1=turns[:], op0=ALU.subtract, op1=ALU.subtract
     )
-    nc.vector.scalar_tensor_tensor(
-        out=angle[:], in0=turns[:], scalar=-TWO_PI_LO, in1=angle[:], op0=ALU.mult, op1=ALU.add
-    )
-    sin_half = work.tile(shape, F32)
-    nc.scalar.activation(out=sin_half[:], in_=angle[:], func=ACT.Sin, scale=0.5)
-    nc.scalar.activation(out=angle[:], in_=angle[:], func=ACT.Abs)
-    nc.vector.tensor_scalar(
-        out=angle[:], in0=angle[:], scalar1=-0.5, scalar2=0.5 * math.pi, op0=ALU.mult, op1=ALU.add
-    )
-    cos_half = work.tile(shape, F32)
-    nc.scalar.activation(out=cos_half[:], in_=angle[:], func=ACT.Sin)
-    emb = work.tile([P, POS_TILES, E], F32)
-    nc.vector.scalar_tensor_tensor(
-        out=emb[:, :, 0:HALF], in0=sin_half[:], scalar=2.0, in1=cos_half[:], op0=ALU.mult, op1=ALU.mult
-    )
-    nc.scalar.activation(out=sin_half[:], in_=sin_half[:], func=ACT.Square)
-    nc.vector.tensor_scalar(
-        out=emb[:, :, HALF:E], in0=sin_half[:], scalar1=-2.0, scalar2=1.0, op0=ALU.mult, op1=ALU.add
-    )
+    emb = work.tile([P, ROUNDS, E], F32)
+    nc.scalar.activation(out=emb[:], in_=minus_f[:], func=ACT.Sin, scale=-2.0 * math.pi)
     nc.scalar.activation(out=sin_tab[:, :, 0:HALF], in_=emb[:, :, 0:HALF], func=ACT.Sin, scale=-1.0)
     nc.scalar.activation(out=sin_tab[:, :, HALF:E], in_=emb[:, :, HALF:E], func=ACT.Sin)
-    nc.vector.tensor_scalar(out=emb[:], in0=emb[:], scalar1=0.5 * math.pi, scalar2=None, op0=ALU.add)
-    nc.scalar.activation(out=cos_tab[:], in_=emb[:], func=ACT.Sin)
+    nc.scalar.activation(out=cos_tab[:], in_=emb[:], func=ACT.Sin, bias=quarter_turn[:])
 
 
 def tile_rotaryembeddingtransformerlayer_pa_t_kernel(
@@ -104,157 +88,237 @@ def tile_rotaryembeddingtransformerlayer_pa_t_kernel(
         tc.tile_pool(name="planes", bufs=1) as plane_pool,
         tc.tile_pool(name="quant", bufs=2) as quant,
         tc.tile_pool(name="mix", bufs=2) as mix,
-        tc.psum_pool(name="psum_t", bufs=4) as psum_t,
-        tc.psum_pool(name="psum_qk", bufs=2) as psum_qk,
-        tc.psum_pool(name="psum_v", bufs=2) as psum_v,
+        tc.psum_pool(name="psum_t", bufs=T_BANKS) as psum_t,
+        tc.psum_pool(name="psum_acc", bufs=4) as psum_acc,
+        tc.manual_schedule(),
     ):
         ident_f32 = const.tile([P, P], F32)
-        make_identity(nc, ident_f32[:])
         ident_bf16 = const.tile([P, P], BF16)
-        make_identity(nc, ident_bf16[:])
         minus_half = const.tile([P, BATCH], F32)
-        nc.vector.memset(minus_half[:], -0.5)
-
-        w_rows = work.tile([P, N_OUT // P, D], BF16)
-        nc.sync.dma_start(out=w_rows[:], in_=Wqkv.rearrange("(r p) k -> p r k", p=P))
-        gain_rows = work.tile([P, P], BF16)
-        nc.vector.memset(gain_rows[:], 0.0)
-        nc.sync.dma_start(out=gain_rows[0:CHUNKS, :], in_=g1.rearrange("(c p) -> c p", p=P))
-        nc.sync.dma_start(out=gain_rows[CHUNKS : 2 * CHUNKS, :], in_=be1.rearrange("(c p) -> c p", p=P))
-        bias_all = const.tile([P, N_OUT], BF16)
-        nc.sync.dma_start(out=bias_all[:], in_=bqkv.partition_broadcast(P))
-
-        gain_ps = psum_t.tile([P, P], BF16, tag="zT")
-        nc.tensor.transpose(gain_ps[:], gain_rows[:], ident_bf16[:])
         gain = const.tile([P, 2 * CHUNKS], F32)
-        nc.vector.tensor_copy(out=gain[:], in_=gain_ps[:, 0 : 2 * CHUNKS])
-
-        w_grouped = work.tile([P, PASSES, N_OUT, PACK], BF16, align_bytes=64)
+        bias_all = const.tile([P, N_OUT], BF16)
         w_codes = const.tile([P, PASSES, N_OUT], U32, align_bytes=64)
         w_scales = const.tile([P, PASSES, N_OUT], U8, align_bytes=64)
-        for c in range(PASSES):
-            for pair in range(N_OUT // (2 * P)):
-                wT = psum_t.tile([P, PACK, 2 * P], BF16, tag="zT")
-                for j in range(PACK):
-                    for h in range(2):
-                        k0 = (PACK * c + j) * P
-                        nc.tensor.transpose(
-                            wT[:, j, h * P : (h + 1) * P], w_rows[:, 2 * pair + h, k0 : k0 + P], ident_bf16[:]
-                        )
-                nc.vector.tensor_copy(
-                    out=w_grouped[:, c, 2 * P * pair : 2 * P * (pair + 1), :],
-                    in_=wT[:].rearrange("p j n -> p n j"),
-                )
-            for lo, hi in ((0, 2 * E), (2 * E, N_OUT)):
-                nc.vector.quantize_mx(
-                    out=w_codes[:, c, lo:hi].bitcast(FP8X4),
-                    scales=w_scales[:, c, lo:hi],
-                    in_=w_grouped[:, c, lo:hi, :].rearrange("p n j -> p (n j)"),
-                )
+        cos_tab = const.tile([P, ROUNDS, E], F32)
+        sin_tab = const.tile([P, ROUNDS, E], F32)
+        w_rows = work.tile([P, N_OUT // P, D], BF16)
+        gain_rows = work.tile([P, P], BF16)
 
-        cos_tab = const.tile([P, POS_TILES, E], F32)
-        sin_tab = const.tile([P, POS_TILES, E], F32)
-        build_position_tables(nc, work, cos_tab, sin_tab)
+        x_of, moments_of, rstd_of, shift_of, z_of, zT_of = {}, {}, {}, {}, {}, {}
+        planes_of, grouped_of, codes_of, scales_of = {}, {}, {}, {}
+        qk_of, straight_of, turned_of = {}, {}, {}
 
-        for t in range(POS_TILES):
-            rows = slice(t * P, (t + 1) * P)
-            x = xin.tile([P, BATCH, D], BF16)
-            nc.sync.dma_start(out=x[:], in_=src[:, rows, :].rearrange("b p k -> p b k"))
+        def live(t):
+            return 0 <= t < ROUNDS
 
-            stats = small.tile([P, BATCH, D // BN_CHUNK, 6], F32)
-            mean_var = small.tile([P, BATCH, 2], F32)
+        def rows(t):
+            return slice(t * P, (t + 1) * P)
+
+        def load(t):
+            x_of[t] = xin.tile([P, BATCH, D], BF16, name="x")
+            nc.sync.dma_start(out=x_of[t][:], in_=src[:, rows(t), :].rearrange("b p k -> p b k"))
+
+        def statistics(t):
+            x = x_of[t]
+            stats = small.tile([P, BATCH, D // BN_CHUNK, 6], F32, name="stats")
+            mean_var = small.tile([P, BATCH, 2], F32, name="mean_var")
             for b in range(BATCH):
                 for h in range(D // BN_CHUNK):
                     nc.vector.bn_stats(out=stats[:, b, h, :], in_=x[:, b, h * BN_CHUNK : (h + 1) * BN_CHUNK])
                 nc.vector.bn_aggr(out=mean_var[:, b, :], in_=stats[:, b, :, :].rearrange("p h s -> p (h s)"))
-            var_eps = small.tile([P, BATCH], F32)
+            var_eps = small.tile([P, BATCH], F32, name="var_eps")
             nc.vector.tensor_scalar(out=var_eps[:], in0=mean_var[:, :, 1], scalar1=EPS, scalar2=None, op0=ALU.add)
-            rstd = small.tile([P, BATCH], F32)
-            nc.gpsimd.tensor_tensor(out=rstd[:], in0=var_eps[:], in1=minus_half[:], op=ALU.pow)
-            shift = small.tile([P, BATCH], F32)
+            moments_of[t] = (mean_var, var_eps)
+
+        def inverse_std(t):
+            rstd_of[t] = small.tile([P, BATCH], F32, name="rstd")
+            nc.gpsimd.tensor_tensor(out=rstd_of[t][:], in0=moments_of[t][1][:], in1=minus_half[:], op=ALU.pow)
+
+        def shift(t):
+            shift_of[t] = small.tile([P, BATCH], F32, name="shift")
             nc.vector.scalar_tensor_tensor(
-                out=shift[:], in0=mean_var[:, :, 0], scalar=-1.0, in1=rstd[:], op0=ALU.mult, op1=ALU.mult
+                out=shift_of[t][:], in0=moments_of[t][0][:, :, 0], scalar=-1.0, in1=rstd_of[t][:],
+                op0=ALU.mult, op1=ALU.mult,
             )
-            z = norm.tile([P, BATCH, D], F32)
-            for b in range(BATCH):
-                nc.scalar.activation(
-                    out=z[:, b, :], in_=x[:, b, :], func=ACT.Identity,
-                    scale=rstd[:, b : b + 1], bias=shift[:, b : b + 1],
-                )
 
-            planes = plane_pool.tile([P, CHUNKS, TOKENS], BF16)
-            for kc in range(CHUNKS):
-                zT = psum_t.tile([P, TOKENS], F32, tag="zT")
-                for b in range(BATCH):
-                    nc.tensor.transpose(zT[:, b * P : (b + 1) * P], z[:, b, kc * P : (kc + 1) * P], ident_f32[:])
-                nc.scalar.activation(
-                    out=planes[:, kc, :], in_=zT[:], func=ACT.Identity,
-                    scale=gain[:, kc : kc + 1], bias=gain[:, CHUNKS + kc : CHUNKS + kc + 1],
-                )
-            grouped = quant.tile([P, PASSES, TOKENS, PACK], BF16, align_bytes=64)
-            codes = quant.tile([P, PASSES, TOKENS], U32, align_bytes=64)
-            scales = quant.tile([P, PASSES, TOKENS], U8, align_bytes=64)
-            for c in range(PASSES):
-                nc.scalar.copy(
-                    out=grouped[:, c, :, :].rearrange("p (m i) j -> p m j i", i=4),
-                    in_=planes[:, PACK * c : PACK * (c + 1), :].rearrange("p j (m i) -> p m j i", i=4),
-                )
-            for c in range(PASSES):
-                nc.vector.quantize_mx(
-                    out=codes[:, c, :].bitcast(FP8X4),
-                    scales=scales[:, c, :],
-                    in_=grouped[:, c, :, :].rearrange("p w j -> p (w j)"),
-                )
-
-            qk = mix.tile([P, BATCH, 2, E], F32)
-            v = mix.tile([P, BATCH, E], F32)
+        def normalise(t):
+            z_of[t] = norm.tile([P, BATCH, D], F32, name="z")
             for b in range(BATCH):
-                tok = slice(b * P, (b + 1) * P)
-                acc_qk = psum_qk.tile([P, 2 * E], F32)
-                for c in range(PASSES):
-                    nc.tensor.matmul_mx(
-                        out=acc_qk[:],
-                        lhsT=codes[:, c, tok].bitcast(FP8X4), lhsT_scale=scales[:, c, tok],
-                        rhs=w_codes[:, c, 0 : 2 * E].bitcast(FP8X4), rhs_scale=w_scales[:, c, 0 : 2 * E],
-                        start=(c == 0), stop=(c == PASSES - 1),
+                scale, bias = rstd_of[t][:, b : b + 1], shift_of[t][:, b : b + 1]
+                if b < BATCH // 2:
+                    nc.scalar.activation(
+                        out=z_of[t][:, b, :], in_=x_of[t][:, b, :], func=ACT.Identity, scale=scale, bias=bias
                     )
+                else:
+                    nc.gpsimd.tensor_scalar(
+                        out=z_of[t][:, b, :], in0=x_of[t][:, b, :], scalar1=scale, scalar2=bias,
+                        op0=ALU.mult, op1=ALU.add,
+                    )
+
+        def transpose(t, kc):
+            zT_of[t, kc] = psum_t.tile([P, TOKENS], F32, name="zT")
+            for b in range(BATCH):
+                nc.tensor.transpose(
+                    zT_of[t, kc][:, b * P : (b + 1) * P], z_of[t][:, b, kc * P : (kc + 1) * P], ident_f32[:]
+                )
+
+        def gain_out(t, kc):
+            if kc == 0:
+                planes_of[t] = plane_pool.tile([P, CHUNKS, TOKENS], BF16, name="planes")
+            nc.scalar.activation(
+                out=planes_of[t][:, kc, :], in_=zT_of[t, kc][:], func=ACT.Identity,
+                scale=gain[:, kc : kc + 1], bias=gain[:, CHUNKS + kc : CHUNKS + kc + 1],
+            )
+
+        def regroup(t, c):
+            if c == 0:
+                grouped_of[t] = quant.tile([P, PASSES, TOKENS, PACK], BF16, name="grouped", align_bytes=64)
+            nc.scalar.copy(
+                out=grouped_of[t][:, c, :, :].rearrange("p (m i) j -> p m j i", i=4),
+                in_=planes_of[t][:, PACK * c : PACK * (c + 1), :].rearrange("p j (m i) -> p m j i", i=4),
+            )
+
+        def quantise(t, c):
+            if c == 0:
+                codes_of[t] = quant.tile([P, PASSES, TOKENS], U32, name="codes", align_bytes=64)
+                scales_of[t] = quant.tile([P, PASSES, TOKENS], U8, name="scales", align_bytes=64)
+            nc.vector.quantize_mx(
+                out=codes_of[t][:, c, :].bitcast(FP8X4),
+                scales=scales_of[t][:, c, :],
+                in_=grouped_of[t][:, c, :, :].rearrange("p w j -> p (w j)"),
+            )
+
+        def multiply(acc, t, b, lo, hi):
+            tok = slice(b * P, (b + 1) * P)
+            for c in range(PASSES):
+                nc.tensor.matmul_mx(
+                    out=acc,
+                    lhsT=codes_of[t][:, c, tok].bitcast(FP8X4), lhsT_scale=scales_of[t][:, c, tok],
+                    rhs=w_codes[:, c, lo:hi].bitcast(FP8X4), rhs_scale=w_scales[:, c, lo:hi],
+                    start=(c == 0), stop=(c == PASSES - 1),
+                )
+
+        def project(t):
+            qk_of[t] = mix.tile([P, BATCH, 2, E], F32, name="qk")
+            v = mix.tile([P, BATCH, E], F32, name="v")
+            for b in range(BATCH):
+                acc_qk = psum_acc.tile([P, 2 * E], F32, name="acc_qk", tag="acc")
+                multiply(acc_qk[:], t, b, 0, 2 * E)
                 nc.vector.tensor_tensor(
-                    out=qk[:, b, :, :].rearrange("p q e -> p (q e)"), in0=acc_qk[:], in1=bias_all[:, 0 : 2 * E],
-                    op=ALU.add,
+                    out=qk_of[t][:, b, :, :].rearrange("p q e -> p (q e)"), in0=acc_qk[:],
+                    in1=bias_all[:, 0 : 2 * E], op=ALU.add,
                 )
                 if b % 2 == 0:
-                    acc_v = psum_v.tile([P, 2, E], F32)
-                for c in range(PASSES):
-                    nc.tensor.matmul_mx(
-                        out=acc_v[:, b % 2, :],
-                        lhsT=codes[:, c, tok].bitcast(FP8X4), lhsT_scale=scales[:, c, tok],
-                        rhs=w_codes[:, c, 2 * E : N_OUT].bitcast(FP8X4), rhs_scale=w_scales[:, c, 2 * E : N_OUT],
-                        start=(c == 0), stop=(c == PASSES - 1),
-                    )
+                    acc_v = psum_acc.tile([P, 2, E], F32, name="acc_v", tag="acc")
+                multiply(acc_v[:, b % 2, :], t, b, 2 * E, N_OUT)
                 if b % 2 == 1:
                     nc.vector.tensor_tensor(
                         out=v[:, b - 1 : b + 1, :], in0=acc_v[:],
                         in1=bias_all[:, 2 * E : N_OUT].unsqueeze(1).to_broadcast([P, 2, E]), op=ALU.add,
                     )
-            nc.sync.dma_start(out=out_2[:, rows, :].rearrange("b p e -> p b e"), in_=v[:])
+            nc.sync.dma_start(out=out_2[:, rows(t), :].rearrange("b p e -> p b e"), in_=v[:])
 
-            straight = mix.tile([P, BATCH, 2, E], F32)
-            turned = mix.tile([P, BATCH, 2, E], F32)
-            nc.gpsimd.tensor_tensor(
-                out=straight[:].rearrange("p b q e -> p (b q) e"),
-                in0=qk[:].rearrange("p b q e -> p (b q) e"),
-                in1=cos_tab[:, t, :].unsqueeze(1).to_broadcast([P, 2 * BATCH, E]),
-                op=ALU.mult,
-            )
-            nc.gpsimd.tensor_tensor(
-                out=turned[:].rearrange("p b q (h i) -> p (b q) h i", h=2),
-                in0=qk[:].rearrange("p b q (i h) -> p (b q) h i", h=2),
-                in1=sin_tab[:, t, :].rearrange("p (h i) -> p h i", h=2).unsqueeze(1).to_broadcast([P, 2 * BATCH, 2, HALF]),
-                op=ALU.mult,
-            )
+        def products(t):
+            straight_of[t] = mix.tile([P, BATCH, 2, E], F32, name="straight")
+            turned_of[t] = mix.tile([P, BATCH, 2, E], F32, name="turned")
+            for b in range(0, BATCH, 2):
+                pair = slice(b, b + 2)
+                nc.gpsimd.tensor_tensor(
+                    out=straight_of[t][:, pair].rearrange("p b q e -> p (b q) e"),
+                    in0=qk_of[t][:, pair].rearrange("p b q e -> p (b q) e"),
+                    in1=cos_tab[:, t, :].unsqueeze(1).to_broadcast([P, 4, E]),
+                    op=ALU.mult,
+                )
+                nc.gpsimd.tensor_tensor(
+                    out=turned_of[t][:, pair].rearrange("p b q (h i) -> p (b q) h i", h=2),
+                    in0=qk_of[t][:, pair].rearrange("p b q (i h) -> p (b q) h i", h=2),
+                    in1=sin_tab[:, t, :].rearrange("p (h i) -> p h i", h=2).unsqueeze(1).to_broadcast([P, 4, 2, HALF]),
+                    op=ALU.mult,
+                )
+
+        def combine(t):
+            straight, turned = straight_of[t], turned_of[t]
             nc.vector.tensor_tensor(out=straight[:, :, 0, :], in0=straight[:, :, 0, :], in1=turned[:, :, 0, :], op=ALU.add)
+            nc.sync.dma_start(out=out_0[:, rows(t), :].rearrange("b p e -> p b e"), in_=straight[:, :, 0, :])
             nc.vector.tensor_tensor(
                 out=straight[:, :, 1, :], in0=straight[:, :, 1, :], in1=turned[:, :, 1, :], op=ALU.subtract
             )
-            nc.sync.dma_start(out=out_0[:, rows, :].rearrange("b p e -> p b e"), in_=straight[:, :, 0, :])
-            nc.sync.dma_start(out=out_1[:, rows, :].rearrange("b p e -> p b e"), in_=straight[:, :, 1, :])
+            nc.sync.dma_start(out=out_1[:, rows(t), :].rearrange("b p e -> p b e"), in_=straight[:, :, 1, :])
+
+        def prepare_gain():
+            gain_ps = psum_acc.tile([P, P], BF16, name="gain_ps", tag="acc")
+            nc.tensor.transpose(gain_ps[:], gain_rows[:], ident_bf16[:])
+            nc.vector.tensor_copy(out=gain[:], in_=gain_ps[:, 0 : 2 * CHUNKS])
+
+        def prepare_weights():
+            w_grouped = work.tile([P, PASSES, N_OUT, PACK], BF16, name="w_grouped", align_bytes=64)
+            for c in range(PASSES):
+                for pair in range(N_OUT // (2 * P)):
+                    wT = psum_acc.tile([P, PACK, 2 * P], BF16, name="wT", tag="acc")
+                    for j in range(PACK):
+                        for h in range(2):
+                            k0 = (PACK * c + j) * P
+                            nc.tensor.transpose(
+                                wT[:, j, h * P : (h + 1) * P], w_rows[:, 2 * pair + h, k0 : k0 + P], ident_bf16[:]
+                            )
+                    nc.vector.tensor_copy(
+                        out=w_grouped[:, c, 2 * P * pair : 2 * P * (pair + 1), :],
+                        in_=wT[:].rearrange("p j n -> p n j"),
+                    )
+            for c in range(PASSES):
+                for lo, hi in ((0, 2 * E), (2 * E, N_OUT)):
+                    nc.vector.quantize_mx(
+                        out=w_codes[:, c, lo:hi].bitcast(FP8X4),
+                        scales=w_scales[:, c, lo:hi],
+                        in_=w_grouped[:, c, lo:hi, :].rearrange("p n j -> p (n j)"),
+                    )
+
+        load(0)
+        nc.vector.memset(gain_rows[:], 0.0)
+        nc.sync.dma_start(out=gain_rows[0:CHUNKS, :], in_=g1.rearrange("(c p) -> c p", p=P))
+        nc.sync.dma_start(out=gain_rows[CHUNKS : 2 * CHUNKS, :], in_=be1.rearrange("(c p) -> c p", p=P))
+        load(1)
+        nc.sync.dma_start(out=w_rows[:], in_=Wqkv.rearrange("(r p) k -> p r k", p=P))
+        nc.sync.dma_start(out=bias_all[:], in_=bqkv.partition_broadcast(P))
+        load(2)
+        make_identity(nc, ident_f32[:])
+        make_identity(nc, ident_bf16[:])
+        nc.vector.memset(minus_half[:], -0.5)
+        build_position_tables(nc, work, cos_tab, sin_tab)
+        prepare_gain()
+
+        for i in range(-2, ROUNDS + 2):
+            if live(i + 3) and i >= 0:
+                load(i + 3)
+            if live(i - 1):
+                quantise(i - 1, 1)
+            if live(i):
+                for kc in range(T_BANKS):
+                    gain_out(i, kc)
+                    transpose(i, kc + T_BANKS)
+            if live(i + 2):
+                statistics(i + 2)
+            if i == 0:
+                prepare_weights()
+            if live(i - 1):
+                project(i - 1)
+            if live(i):
+                for kc in range(T_BANKS, CHUNKS):
+                    gain_out(i, kc)
+            if live(i + 1):
+                normalise(i + 1)
+                for kc in range(T_BANKS):
+                    transpose(i + 1, kc)
+            if live(i + 2):
+                inverse_std(i + 2)
+            if live(i - 1):
+                products(i - 1)
+            if live(i):
+                regroup(i, 0)
+                regroup(i, 1)
+            if live(i - 2):
+                combine(i - 2)
+            if live(i + 2):
+                shift(i + 2)
+            if live(i):
+                quantise(i, 0)

@@ -145,15 +145,9 @@ def tile_rotaryembeddingtransformerlayer_pa_t_kernel(
             z_of[t] = norm.tile([P, BATCH, D], F32, name="z")
             for b in range(BATCH):
                 scale, bias = rstd_of[t][:, b : b + 1], shift_of[t][:, b : b + 1]
-                if b < BATCH // 2:
-                    nc.scalar.activation(
-                        out=z_of[t][:, b, :], in_=x_of[t][:, b, :], func=ACT.Identity, scale=scale, bias=bias
-                    )
-                else:
-                    nc.gpsimd.tensor_scalar(
-                        out=z_of[t][:, b, :], in0=x_of[t][:, b, :], scalar1=scale, scalar2=bias,
-                        op0=ALU.mult, op1=ALU.add,
-                    )
+                nc.scalar.activation(
+                    out=z_of[t][:, b, :], in_=x_of[t][:, b, :], func=ACT.Identity, scale=scale, bias=bias
+                )
 
         def transpose(t, kc):
             zT_of[t, kc] = psum_t.tile([P, TOKENS], F32, name="zT")
@@ -223,13 +217,13 @@ def tile_rotaryembeddingtransformerlayer_pa_t_kernel(
             turned_of[t] = mix.tile([P, BATCH, 2, E], F32, name="turned")
             for b in range(0, BATCH, 2):
                 pair = slice(b, b + 2)
-                nc.gpsimd.tensor_tensor(
+                nc.vector.tensor_tensor(
                     out=straight_of[t][:, pair].rearrange("p b q e -> p (b q) e"),
                     in0=qk_of[t][:, pair].rearrange("p b q e -> p (b q) e"),
                     in1=cos_tab[:, t, :].unsqueeze(1).to_broadcast([P, 4, E]),
                     op=ALU.mult,
                 )
-                nc.gpsimd.tensor_tensor(
+                nc.vector.tensor_tensor(
                     out=turned_of[t][:, pair].rearrange("p b q (h i) -> p (b q) h i", h=2),
                     in0=qk_of[t][:, pair].rearrange("p b q (i h) -> p (b q) h i", h=2),
                     in1=sin_tab[:, t, :].rearrange("p (h i) -> p h i", h=2).unsqueeze(1).to_broadcast([P, 4, 2, HALF]),

@@ -28,7 +28,7 @@ CHUNKS = D // P
 ROUNDS = SEQ // P
 TOKENS = BATCH * P
 BN_CHUNK = 512
-T_BANKS = 4
+T_BANKS = 3
 
 FREQ_RATIO = 10000.0 ** (-1.0 / HALF)
 ROUND_MAGIC = 12582912.0
@@ -90,6 +90,7 @@ def tile_rotaryembeddingtransformerlayer_pa_t_kernel(
         tc.tile_pool(name="mix", bufs=2) as mix,
         tc.psum_pool(name="psum_t", bufs=T_BANKS) as psum_t,
         tc.psum_pool(name="psum_acc", bufs=4) as psum_acc,
+        tc.psum_pool(name="psum_cos", bufs=1) as psum_cos,
         tc.manual_schedule(),
     ):
         ident_f32 = const.tile([P, P], F32)
@@ -106,7 +107,7 @@ def tile_rotaryembeddingtransformerlayer_pa_t_kernel(
 
         x_of, moments_of, rstd_of, shift_of, z_of, zT_of = {}, {}, {}, {}, {}, {}
         planes_of, grouped_of, codes_of, scales_of = {}, {}, {}, {}
-        qk_of, straight_of, turned_of = {}, {}, {}
+        qk_of, straight_of = {}, {}
 
         def live(t):
             return 0 <= t < ROUNDS
@@ -126,28 +127,35 @@ def tile_rotaryembeddingtransformerlayer_pa_t_kernel(
                 for h in range(D // BN_CHUNK):
                     nc.vector.bn_stats(out=stats[:, b, h, :], in_=x[:, b, h * BN_CHUNK : (h + 1) * BN_CHUNK])
                 nc.vector.bn_aggr(out=mean_var[:, b, :], in_=stats[:, b, :, :].rearrange("p h s -> p (h s)"))
+            moments_of[t] = mean_var
+
+        def scale_and_shift(t):
             var_eps = small.tile([P, BATCH], F32, name="var_eps")
-            nc.vector.tensor_scalar(out=var_eps[:], in0=mean_var[:, :, 1], scalar1=EPS, scalar2=None, op0=ALU.add)
-            moments_of[t] = (mean_var, var_eps)
-
-        def inverse_std(t):
-            rstd_of[t] = small.tile([P, BATCH], F32, name="rstd")
-            nc.gpsimd.tensor_tensor(out=rstd_of[t][:], in0=moments_of[t][1][:], in1=minus_half[:], op=ALU.pow)
-
-        def shift(t):
-            shift_of[t] = small.tile([P, BATCH], F32, name="shift")
-            nc.vector.scalar_tensor_tensor(
-                out=shift_of[t][:], in0=moments_of[t][0][:, :, 0], scalar=-1.0, in1=rstd_of[t][:],
-                op0=ALU.mult, op1=ALU.mult,
+            nc.gpsimd.tensor_scalar(
+                out=var_eps[:], in0=moments_of[t][:, :, 1], scalar1=1.0, scalar2=EPS, op0=ALU.mult, op1=ALU.add
             )
+            minus_mean = small.tile([P, BATCH], F32, name="minus_mean")
+            nc.gpsimd.tensor_scalar(
+                out=minus_mean[:], in0=moments_of[t][:, :, 0], scalar1=-1.0, scalar2=0.0, op0=ALU.mult, op1=ALU.add
+            )
+            rstd_of[t] = small.tile([P, BATCH], F32, name="rstd")
+            nc.gpsimd.tensor_tensor(out=rstd_of[t][:], in0=var_eps[:], in1=minus_half[:], op=ALU.pow)
+            shift_of[t] = small.tile([P, BATCH], F32, name="shift")
+            nc.gpsimd.tensor_tensor(out=shift_of[t][:], in0=minus_mean[:], in1=rstd_of[t][:], op=ALU.mult)
 
         def normalise(t):
             z_of[t] = norm.tile([P, BATCH, D], F32, name="z")
             for b in range(BATCH):
                 scale, bias = rstd_of[t][:, b : b + 1], shift_of[t][:, b : b + 1]
-                nc.scalar.activation(
-                    out=z_of[t][:, b, :], in_=x_of[t][:, b, :], func=ACT.Identity, scale=scale, bias=bias
-                )
+                if b < BATCH - 1:
+                    nc.scalar.activation(
+                        out=z_of[t][:, b, :], in_=x_of[t][:, b, :], func=ACT.Identity, scale=scale, bias=bias
+                    )
+                else:
+                    nc.gpsimd.tensor_scalar(
+                        out=z_of[t][:, b, :], in0=x_of[t][:, b, :], scalar1=scale, scalar2=bias,
+                        op0=ALU.mult, op1=ALU.add,
+                    )
 
         def transpose(t, kc):
             zT_of[t, kc] = psum_t.tile([P, TOKENS], F32, name="zT")
@@ -193,7 +201,10 @@ def tile_rotaryembeddingtransformerlayer_pa_t_kernel(
                 )
 
         def project(t):
+            cos_ps = psum_cos.tile([P, E], F32, name="cos_ps")
+            nc.tensor.matmul(out=cos_ps[:], lhsT=ident_f32[:], rhs=cos_tab[:, t, :], start=True, stop=True)
             qk_of[t] = mix.tile([P, BATCH, 2, E], F32, name="qk")
+            straight_of[t] = mix.tile([P, BATCH, 2, E], F32, name="straight")
             v = mix.tile([P, BATCH, E], F32, name="v")
             for b in range(BATCH):
                 acc_qk = psum_acc.tile([P, 2 * E], F32, name="acc_qk", tag="acc")
@@ -206,35 +217,33 @@ def tile_rotaryembeddingtransformerlayer_pa_t_kernel(
                     acc_v = psum_acc.tile([P, 2, E], F32, name="acc_v", tag="acc")
                 multiply(acc_v[:, b % 2, :], t, b, 2 * E, N_OUT)
                 if b % 2 == 1:
+                    pair = slice(b - 1, b + 1)
                     nc.vector.tensor_tensor(
-                        out=v[:, b - 1 : b + 1, :], in0=acc_v[:],
+                        out=v[:, pair, :], in0=acc_v[:],
                         in1=bias_all[:, 2 * E : N_OUT].unsqueeze(1).to_broadcast([P, 2, E]), op=ALU.add,
+                    )
+                    nc.vector.tensor_tensor(
+                        out=straight_of[t][:, pair].rearrange("p b q e -> p (b q) e"),
+                        in0=qk_of[t][:, pair].rearrange("p b q e -> p (b q) e"),
+                        in1=cos_ps[:].unsqueeze(1).to_broadcast([P, 4, E]),
+                        op=ALU.mult,
                     )
             nc.sync.dma_start(out=out_2[:, rows(t), :].rearrange("b p e -> p b e"), in_=v[:])
 
-        def products(t):
-            straight_of[t] = mix.tile([P, BATCH, 2, E], F32, name="straight")
-            turned_of[t] = mix.tile([P, BATCH, 2, E], F32, name="turned")
+        def finish_mix(t):
+            straight = straight_of[t]
+            turned = mix.tile([P, BATCH, 2, E], F32, name="turned")
             for b in range(0, BATCH, 2):
                 pair = slice(b, b + 2)
-                nc.vector.tensor_tensor(
-                    out=straight_of[t][:, pair].rearrange("p b q e -> p (b q) e"),
-                    in0=qk_of[t][:, pair].rearrange("p b q e -> p (b q) e"),
-                    in1=cos_tab[:, t, :].unsqueeze(1).to_broadcast([P, 4, E]),
-                    op=ALU.mult,
-                )
-                nc.vector.tensor_tensor(
-                    out=turned_of[t][:, pair].rearrange("p b q (h i) -> p (b q) h i", h=2),
+                nc.gpsimd.tensor_tensor(
+                    out=turned[:, pair].rearrange("p b q (h i) -> p (b q) h i", h=2),
                     in0=qk_of[t][:, pair].rearrange("p b q (i h) -> p (b q) h i", h=2),
                     in1=sin_tab[:, t, :].rearrange("p (h i) -> p h i", h=2).unsqueeze(1).to_broadcast([P, 4, 2, HALF]),
                     op=ALU.mult,
                 )
-
-        def combine(t):
-            straight, turned = straight_of[t], turned_of[t]
-            nc.vector.tensor_tensor(out=straight[:, :, 0, :], in0=straight[:, :, 0, :], in1=turned[:, :, 0, :], op=ALU.add)
+            nc.gpsimd.tensor_tensor(out=straight[:, :, 0, :], in0=straight[:, :, 0, :], in1=turned[:, :, 0, :], op=ALU.add)
             nc.sync.dma_start(out=out_0[:, rows(t), :].rearrange("b p e -> p b e"), in_=straight[:, :, 0, :])
-            nc.vector.tensor_tensor(
+            nc.gpsimd.tensor_tensor(
                 out=straight[:, :, 1, :], in0=straight[:, :, 1, :], in1=turned[:, :, 1, :], op=ALU.subtract
             )
             nc.sync.dma_start(out=out_1[:, rows(t), :].rearrange("b p e -> p b e"), in_=straight[:, :, 1, :])
@@ -281,13 +290,14 @@ def tile_rotaryembeddingtransformerlayer_pa_t_kernel(
         build_position_tables(nc, work, cos_tab, sin_tab)
         prepare_gain()
 
-        for i in range(-2, ROUNDS + 2):
+        for i in range(-2, ROUNDS + 1):
             if live(i + 3) and i >= 0:
                 load(i + 3)
             if live(i - 1):
+                quantise(i - 1, 0)
                 quantise(i - 1, 1)
             if live(i):
-                for kc in range(T_BANKS):
+                for kc in range(CHUNKS - T_BANKS):
                     gain_out(i, kc)
                     transpose(i, kc + T_BANKS)
             if live(i + 2):
@@ -297,22 +307,16 @@ def tile_rotaryembeddingtransformerlayer_pa_t_kernel(
             if live(i - 1):
                 project(i - 1)
             if live(i):
-                for kc in range(T_BANKS, CHUNKS):
+                for kc in range(CHUNKS - T_BANKS, CHUNKS):
                     gain_out(i, kc)
             if live(i + 1):
                 normalise(i + 1)
                 for kc in range(T_BANKS):
                     transpose(i + 1, kc)
             if live(i + 2):
-                inverse_std(i + 2)
+                scale_and_shift(i + 2)
             if live(i - 1):
-                products(i - 1)
+                finish_mix(i - 1)
             if live(i):
                 regroup(i, 0)
                 regroup(i, 1)
-            if live(i - 2):
-                combine(i - 2)
-            if live(i + 2):
-                shift(i + 2)
-            if live(i):
-                quantise(i, 0)

@@ -36,43 +36,34 @@ ROUND_MAGIC = 12582912.0
 FLOPS = 2 * BATCH * SEQ * D * N_OUT
 
 
-def build_position_tables(nc, work, cos_tab, sin_tab):
-    freq = work.tile([P, HALF], F32)
-    nc.vector.memset(freq[:, 0:1], 1.0)
-    nc.vector.tensor_scalar(out=freq[:, 0:1], in0=freq[:, 0:1], scalar1=0.5 / math.pi, scalar2=None, op0=ALU.mult)
-    for doubling in range(7):
-        n = 2**doubling
-        nc.vector.tensor_scalar(
-            out=freq[:, n : 2 * n], in0=freq[:, 0:n], scalar1=FREQ_RATIO**n, scalar2=None, op0=ALU.mult
-        )
+def build_position_tables(nc, work, tables):
     quarter_turn = work.tile([P, 1], F32)
     nc.vector.memset(quarter_turn[:], 1.0)
     nc.vector.tensor_scalar(out=quarter_turn[:], in0=quarter_turn[:], scalar1=0.5 * math.pi, scalar2=None, op0=ALU.mult)
-    pos_int = work.tile([P, ROUNDS], I32)
-    nc.gpsimd.iota(pos_int[:], pattern=[[P, ROUNDS]], base=0, channel_multiplier=1)
-    pos = work.tile([P, ROUNDS], F32)
-    nc.vector.tensor_copy(out=pos[:], in_=pos_int[:])
-
-    turns = work.tile([P, ROUNDS, E], F32)
-    half_shape = [P, ROUNDS, HALF]
-    nc.vector.tensor_tensor(
-        out=turns[:, :, 0:HALF],
-        in0=freq[:].unsqueeze(1).to_broadcast(half_shape),
-        in1=pos[:].unsqueeze(2).to_broadcast(half_shape),
-        op=ALU.mult,
-    )
-    nc.vector.tensor_scalar(out=turns[:, :, HALF:E], in0=turns[:, :, 0:HALF], scalar1=0.25, scalar2=None, op0=ALU.add)
-    whole = work.tile([P, ROUNDS, E], F32)
+    position = work.tile([P, ROUNDS, 1], I32)
+    nc.gpsimd.iota(position[:], pattern=[[P, ROUNDS]], base=0, channel_multiplier=1)
+    turns = work.tile([P, ROUNDS, HALF], F32)
+    nc.vector.tensor_scalar(out=turns[:, :, 0:1], in0=position[:], scalar1=0.5 / math.pi, scalar2=None, op0=ALU.mult)
+    for doubling in range(7):
+        n = 2**doubling
+        nc.vector.tensor_scalar(
+            out=turns[:, :, n : 2 * n], in0=turns[:, :, 0:n], scalar1=FREQ_RATIO**n, scalar2=None, op0=ALU.mult
+        )
+    whole = work.tile([P, ROUNDS, HALF], F32)
     nc.vector.tensor_scalar(out=whole[:], in0=turns[:], scalar1=ROUND_MAGIC, scalar2=None, op0=ALU.add)
-    minus_f = work.tile([P, ROUNDS, E], F32)
+    minus_f = work.tile([P, ROUNDS, HALF], F32)
     nc.vector.scalar_tensor_tensor(
         out=minus_f[:], in0=whole[:], scalar=ROUND_MAGIC, in1=turns[:], op0=ALU.subtract, op1=ALU.subtract
     )
     emb = work.tile([P, ROUNDS, E], F32)
-    nc.scalar.activation(out=emb[:], in_=minus_f[:], func=ACT.Sin, scale=-2.0 * math.pi)
-    nc.scalar.activation(out=sin_tab[:, :, 0:HALF], in_=emb[:, :, 0:HALF], func=ACT.Sin, scale=-1.0)
-    nc.scalar.activation(out=sin_tab[:, :, HALF:E], in_=emb[:, :, HALF:E], func=ACT.Sin)
-    nc.scalar.activation(out=cos_tab[:], in_=emb[:], func=ACT.Sin, bias=quarter_turn[:])
+    nc.scalar.activation(out=emb[:, :, 0:HALF], in_=minus_f[:], func=ACT.Sin, scale=-2.0 * math.pi)
+    nc.scalar.activation(out=minus_f[:], in_=minus_f[:], func=ACT.Abs)
+    nc.scalar.activation(
+        out=emb[:, :, HALF:E], in_=minus_f[:], func=ACT.Sin, scale=-2.0 * math.pi, bias=quarter_turn[:]
+    )
+    nc.scalar.activation(out=tables[:, :, 0, :], in_=emb[:], func=ACT.Sin, bias=quarter_turn[:])
+    nc.scalar.activation(out=tables[:, :, 1, 0:HALF], in_=emb[:, :, 0:HALF], func=ACT.Sin, scale=-1.0)
+    nc.scalar.activation(out=tables[:, :, 1, HALF:E], in_=emb[:, :, HALF:E], func=ACT.Sin)
 
 
 def tile_rotaryembeddingtransformerlayer_pa_t_kernel(
@@ -90,7 +81,7 @@ def tile_rotaryembeddingtransformerlayer_pa_t_kernel(
         tc.tile_pool(name="mix", bufs=2) as mix,
         tc.psum_pool(name="psum_t", bufs=T_BANKS) as psum_t,
         tc.psum_pool(name="psum_acc", bufs=4) as psum_acc,
-        tc.psum_pool(name="psum_cos", bufs=1) as psum_cos,
+        tc.psum_pool(name="psum_tab", bufs=1) as psum_tab,
         tc.manual_schedule(),
     ):
         ident_f32 = const.tile([P, P], F32)
@@ -100,14 +91,13 @@ def tile_rotaryembeddingtransformerlayer_pa_t_kernel(
         bias_all = const.tile([P, N_OUT], BF16)
         w_codes = const.tile([P, PASSES, N_OUT], U32, align_bytes=64)
         w_scales = const.tile([P, PASSES, N_OUT], U8, align_bytes=64)
-        cos_tab = const.tile([P, ROUNDS, E], F32)
-        sin_tab = const.tile([P, ROUNDS, E], F32)
+        tables = const.tile([P, ROUNDS, 2, E], F32)
         w_rows = work.tile([P, N_OUT // P, D], BF16)
         gain_rows = work.tile([P, P], BF16)
 
         x_of, moments_of, rstd_of, shift_of, z_of, zT_of = {}, {}, {}, {}, {}, {}
         planes_of, grouped_of, codes_of, scales_of = {}, {}, {}, {}
-        qk_of, straight_of = {}, {}
+        qk_of, straight_of, turned_of = {}, {}, {}
 
         def live(t):
             return 0 <= t < ROUNDS
@@ -180,14 +170,13 @@ def tile_rotaryembeddingtransformerlayer_pa_t_kernel(
                 in_=planes_of[t][:, PACK * c : PACK * (c + 1), :].rearrange("p j (m i) -> p m j i", i=4),
             )
 
-        def quantise(t, c):
-            if c == 0:
-                codes_of[t] = quant.tile([P, PASSES, TOKENS], U32, name="codes", align_bytes=64)
-                scales_of[t] = quant.tile([P, PASSES, TOKENS], U8, name="scales", align_bytes=64)
+        def quantise(t):
+            codes_of[t] = quant.tile([P, PASSES, TOKENS], U32, name="codes", align_bytes=64)
+            scales_of[t] = quant.tile([P, PASSES, TOKENS], U8, name="scales", align_bytes=64)
             nc.vector.quantize_mx(
-                out=codes_of[t][:, c, :].bitcast(FP8X4),
-                scales=scales_of[t][:, c, :],
-                in_=grouped_of[t][:, c, :, :].rearrange("p w j -> p (w j)"),
+                out=codes_of[t][:].rearrange("p c w -> p (c w)").bitcast(FP8X4),
+                scales=scales_of[t][:].rearrange("p c w -> p (c w)"),
+                in_=grouped_of[t][:].rearrange("p c w j -> p (c w j)"),
             )
 
         def multiply(acc, t, b, lo, hi):
@@ -200,11 +189,23 @@ def tile_rotaryembeddingtransformerlayer_pa_t_kernel(
                     start=(c == 0), stop=(c == PASSES - 1),
                 )
 
+        def turn(engine, t, pair, sines):
+            engine.tensor_tensor(
+                out=turned_of[t][:, pair].rearrange("p b q (h i) -> p (b q) h i", h=2),
+                in0=qk_of[t][:, pair].rearrange("p b q (i h) -> p (b q) h i", h=2),
+                in1=sines.rearrange("p (h i) -> p h i", h=2).unsqueeze(1).to_broadcast([P, 4, 2, HALF]),
+                op=ALU.mult,
+            )
+
         def project(t):
-            cos_ps = psum_cos.tile([P, E], F32, name="cos_ps")
-            nc.tensor.matmul(out=cos_ps[:], lhsT=ident_f32[:], rhs=cos_tab[:, t, :], start=True, stop=True)
+            tab_ps = psum_tab.tile([P, 2, E], F32, name="tab_ps")
+            nc.tensor.matmul(
+                out=tab_ps[:].rearrange("p s e -> p (s e)"), lhsT=ident_f32[:],
+                rhs=tables[:, t, :, :].rearrange("p s e -> p (s e)"), start=True, stop=True,
+            )
             qk_of[t] = mix.tile([P, BATCH, 2, E], F32, name="qk")
             straight_of[t] = mix.tile([P, BATCH, 2, E], F32, name="straight")
+            turned_of[t] = mix.tile([P, BATCH, 2, E], F32, name="turned")
             v = mix.tile([P, BATCH, E], F32, name="v")
             for b in range(BATCH):
                 acc_qk = psum_acc.tile([P, 2 * E], F32, name="acc_qk", tag="acc")
@@ -225,28 +226,24 @@ def tile_rotaryembeddingtransformerlayer_pa_t_kernel(
                     nc.vector.tensor_tensor(
                         out=straight_of[t][:, pair].rearrange("p b q e -> p (b q) e"),
                         in0=qk_of[t][:, pair].rearrange("p b q e -> p (b q) e"),
-                        in1=cos_ps[:].unsqueeze(1).to_broadcast([P, 4, E]),
+                        in1=tab_ps[:, 0, :].unsqueeze(1).to_broadcast([P, 4, E]),
                         op=ALU.mult,
                     )
+            turn(nc.vector, t, slice(2, 4), tab_ps[:, 1, :])
             nc.sync.dma_start(out=out_2[:, rows(t), :].rearrange("b p e -> p b e"), in_=v[:])
 
         def finish_mix(t):
-            straight = straight_of[t]
-            turned = mix.tile([P, BATCH, 2, E], F32, name="turned")
+            straight, turned = straight_of[t], turned_of[t]
+            turn(nc.gpsimd, t, slice(0, 2), tables[:, t, 1, :])
             for b in range(0, BATCH, 2):
                 pair = slice(b, b + 2)
-                nc.gpsimd.tensor_tensor(
-                    out=turned[:, pair].rearrange("p b q (h i) -> p (b q) h i", h=2),
-                    in0=qk_of[t][:, pair].rearrange("p b q (i h) -> p (b q) h i", h=2),
-                    in1=sin_tab[:, t, :].rearrange("p (h i) -> p h i", h=2).unsqueeze(1).to_broadcast([P, 4, 2, HALF]),
-                    op=ALU.mult,
-                )
-            nc.gpsimd.tensor_tensor(out=straight[:, :, 0, :], in0=straight[:, :, 0, :], in1=turned[:, :, 0, :], op=ALU.add)
-            nc.sync.dma_start(out=out_0[:, rows(t), :].rearrange("b p e -> p b e"), in_=straight[:, :, 0, :])
-            nc.gpsimd.tensor_tensor(
-                out=straight[:, :, 1, :], in0=straight[:, :, 1, :], in1=turned[:, :, 1, :], op=ALU.subtract
-            )
-            nc.sync.dma_start(out=out_1[:, rows(t), :].rearrange("b p e -> p b e"), in_=straight[:, :, 1, :])
+                for q, out, op in ((0, out_0, ALU.add), (1, out_1, ALU.subtract)):
+                    nc.gpsimd.tensor_tensor(
+                        out=straight[:, pair, q, :], in0=straight[:, pair, q, :], in1=turned[:, pair, q, :], op=op
+                    )
+                    nc.sync.dma_start(
+                        out=out[pair, rows(t), :].rearrange("b p e -> p b e"), in_=straight[:, pair, q, :]
+                    )
 
         def prepare_gain():
             gain_ps = psum_acc.tile([P, P], BF16, name="gain_ps", tag="acc")
@@ -287,15 +284,14 @@ def tile_rotaryembeddingtransformerlayer_pa_t_kernel(
         make_identity(nc, ident_f32[:])
         make_identity(nc, ident_bf16[:])
         nc.vector.memset(minus_half[:], -0.5)
-        build_position_tables(nc, work, cos_tab, sin_tab)
+        build_position_tables(nc, work, tables)
         prepare_gain()
 
         for i in range(-2, ROUNDS + 1):
             if live(i + 3) and i >= 0:
                 load(i + 3)
             if live(i - 1):
-                quantise(i - 1, 0)
-                quantise(i - 1, 1)
+                quantise(i - 1)
             if live(i):
                 for kc in range(CHUNKS - T_BANKS):
                     gain_out(i, kc)

@@ -28,7 +28,7 @@ CHUNKS = D // P
 ROUNDS = SEQ // P
 TOKENS = BATCH * P
 BN_CHUNK = 512
-T_BANKS = 3
+T_BANKS = 4
 
 FREQ_RATIO = 10000.0 ** (-1.0 / HALF)
 ROUND_MAGIC = 12582912.0
@@ -80,7 +80,7 @@ def tile_rotaryembeddingtransformerlayer_pa_t_kernel(
         tc.tile_pool(name="quant", bufs=2) as quant,
         tc.tile_pool(name="mix", bufs=2) as mix,
         tc.psum_pool(name="psum_t", bufs=T_BANKS) as psum_t,
-        tc.psum_pool(name="psum_acc", bufs=4) as psum_acc,
+        tc.psum_pool(name="psum_acc", bufs=3) as psum_acc,
         tc.psum_pool(name="psum_tab", bufs=1) as psum_tab,
         tc.manual_schedule(),
     ):
@@ -116,6 +116,7 @@ def tile_rotaryembeddingtransformerlayer_pa_t_kernel(
             for b in range(BATCH):
                 for h in range(D // BN_CHUNK):
                     nc.vector.bn_stats(out=stats[:, b, h, :], in_=x[:, b, h * BN_CHUNK : (h + 1) * BN_CHUNK])
+            for b in range(BATCH):
                 nc.vector.bn_aggr(out=mean_var[:, b, :], in_=stats[:, b, :, :].rearrange("p h s -> p (h s)"))
             moments_of[t] = mean_var
 
@@ -133,19 +134,20 @@ def tile_rotaryembeddingtransformerlayer_pa_t_kernel(
             shift_of[t] = small.tile([P, BATCH], F32, name="shift")
             nc.gpsimd.tensor_tensor(out=shift_of[t][:], in0=minus_mean[:], in1=rstd_of[t][:], op=ALU.mult)
 
-        def normalise(t):
+        def normalise_last(t):
             z_of[t] = norm.tile([P, BATCH, D], F32, name="z")
-            for b in range(BATCH):
-                scale, bias = rstd_of[t][:, b : b + 1], shift_of[t][:, b : b + 1]
-                if b < BATCH - 1:
-                    nc.scalar.activation(
-                        out=z_of[t][:, b, :], in_=x_of[t][:, b, :], func=ACT.Identity, scale=scale, bias=bias
-                    )
-                else:
-                    nc.gpsimd.tensor_scalar(
-                        out=z_of[t][:, b, :], in0=x_of[t][:, b, :], scalar1=scale, scalar2=bias,
-                        op0=ALU.mult, op1=ALU.add,
-                    )
+            b = BATCH - 1
+            nc.gpsimd.tensor_scalar(
+                out=z_of[t][:, b, :], in0=x_of[t][:, b, :], scalar1=rstd_of[t][:, b : b + 1],
+                scalar2=shift_of[t][:, b : b + 1], op0=ALU.mult, op1=ALU.add,
+            )
+
+        def normalise(t):
+            for b in range(BATCH - 1):
+                nc.scalar.activation(
+                    out=z_of[t][:, b, :], in_=x_of[t][:, b, :], func=ACT.Identity,
+                    scale=rstd_of[t][:, b : b + 1], bias=shift_of[t][:, b : b + 1],
+                )
 
         def transpose(t, kc):
             zT_of[t, kc] = psum_t.tile([P, TOKENS], F32, name="zT")
@@ -311,6 +313,7 @@ def tile_rotaryembeddingtransformerlayer_pa_t_kernel(
                     transpose(i + 1, kc)
             if live(i + 2):
                 scale_and_shift(i + 2)
+                normalise_last(i + 2)
             if live(i - 1):
                 finish_mix(i - 1)
             if live(i):

@@ -29,6 +29,8 @@ ROUNDS = SEQ // P
 TOKENS = BATCH * P
 BN_CHUNK = 512
 T_BANKS = 4
+NORM_ON_GPSIMD = 2
+TURN_ON_VECTOR = 2
 
 FREQ_RATIO = 10000.0 ** (-1.0 / HALF)
 ROUND_MAGIC = 12582912.0
@@ -136,14 +138,14 @@ def tile_rotaryembeddingtransformerlayer_pa_t_kernel(
 
         def normalise_last(t):
             z_of[t] = norm.tile([P, BATCH, D], F32, name="z")
-            b = BATCH - 1
-            nc.gpsimd.tensor_scalar(
-                out=z_of[t][:, b, :], in0=x_of[t][:, b, :], scalar1=rstd_of[t][:, b : b + 1],
-                scalar2=shift_of[t][:, b : b + 1], op0=ALU.mult, op1=ALU.add,
-            )
+            for b in range(BATCH - NORM_ON_GPSIMD, BATCH):
+                nc.gpsimd.tensor_scalar(
+                    out=z_of[t][:, b, :], in0=x_of[t][:, b, :], scalar1=rstd_of[t][:, b : b + 1],
+                    scalar2=shift_of[t][:, b : b + 1], op0=ALU.mult, op1=ALU.add,
+                )
 
         def normalise(t):
-            for b in range(BATCH - 1):
+            for b in range(BATCH - NORM_ON_GPSIMD):
                 nc.scalar.activation(
                     out=z_of[t][:, b, :], in_=x_of[t][:, b, :], func=ACT.Identity,
                     scale=rstd_of[t][:, b : b + 1], bias=shift_of[t][:, b : b + 1],
@@ -191,11 +193,11 @@ def tile_rotaryembeddingtransformerlayer_pa_t_kernel(
                     start=(c == 0), stop=(c == PASSES - 1),
                 )
 
-        def turn(engine, t, pair, sines):
+        def turn(engine, t, first, last, sines):
             engine.tensor_tensor(
-                out=turned_of[t][:, pair].rearrange("p b q (h i) -> p (b q) h i", h=2),
-                in0=qk_of[t][:, pair].rearrange("p b q (i h) -> p (b q) h i", h=2),
-                in1=sines.rearrange("p (h i) -> p h i", h=2).unsqueeze(1).to_broadcast([P, 4, 2, HALF]),
+                out=turned_of[t][:, first:last].rearrange("p b q (h i) -> p (b q) h i", h=2),
+                in0=qk_of[t][:, first:last].rearrange("p b q (i h) -> p (b q) h i", h=2),
+                in1=sines.rearrange("p (h i) -> p h i", h=2).unsqueeze(1).to_broadcast([P, 2 * (last - first), 2, HALF]),
                 op=ALU.mult,
             )
 
@@ -231,12 +233,12 @@ def tile_rotaryembeddingtransformerlayer_pa_t_kernel(
                         in1=tab_ps[:, 0, :].unsqueeze(1).to_broadcast([P, 4, E]),
                         op=ALU.mult,
                     )
-            turn(nc.vector, t, slice(2, 4), tab_ps[:, 1, :])
+            turn(nc.vector, t, BATCH - TURN_ON_VECTOR, BATCH, tab_ps[:, 1, :])
             nc.sync.dma_start(out=out_2[:, rows(t), :].rearrange("b p e -> p b e"), in_=v[:])
 
         def finish_mix(t):
             straight, turned = straight_of[t], turned_of[t]
-            turn(nc.gpsimd, t, slice(0, 2), tables[:, t, 1, :])
+            turn(nc.gpsimd, t, 0, BATCH - TURN_ON_VECTOR, tables[:, t, 1, :])
             for b in range(0, BATCH, 2):
                 pair = slice(b, b + 2)
                 for q, out, op in ((0, out_0, ALU.add), (1, out_1, ALU.subtract)):

import math

import concourse.mybir as mybir
from concourse.masks import make_identity

F32 = mybir.dt.float32
BF16 = mybir.dt.bfloat16
I32 = mybir.dt.int32
U32 = mybir.dt.uint32
U8 = mybir.dt.uint8
FP8X4 = mybir.dt.float8_e4m3fn_x4
ALU = mybir.AluOpType
ACT = mybir.ActivationFunctionType

P = 128
BATCH = 4
SEQ = 1024
D = 1024
E = 256
HALF = E // 2
N_OUT = 3 * E
EPS = 1e-5

PACK = 4
K_PASS = P * PACK
PASSES = D // K_PASS
CHUNKS = D // P
ROUNDS = SEQ // P
TOKENS = BATCH * P
BN_CHUNK = 512
T_BANKS = 4
NORM_ON_GPSIMD = 2
TURN_ON_VECTOR = 2

FREQ_RATIO = 10000.0 ** (-1.0 / HALF)
ROUND_MAGIC = 12582912.0

FLOPS = 2 * BATCH * SEQ * D * N_OUT


def build_position_tables(nc, work, tables):
    quarter_turn = work.tile([P, 1], F32)
    nc.vector.memset(quarter_turn[:], 1.0)
    nc.vector.tensor_scalar(out=quarter_turn[:], in0=quarter_turn[:], scalar1=0.5 * math.pi, scalar2=None, op0=ALU.mult)
    position = work.tile([P, ROUNDS, 1], I32)
    nc.gpsimd.iota(position[:], pattern=[[P, ROUNDS]], base=0, channel_multiplier=1)
    turns = work.tile([P, ROUNDS, HALF], F32)
    nc.vector.tensor_scalar(out=turns[:, :, 0:1], in0=position[:], scalar1=0.5 / math.pi, scalar2=None, op0=ALU.mult)
    for doubling in range(7):
        n = 2**doubling
        nc.vector.tensor_scalar(
            out=turns[:, :, n : 2 * n], in0=turns[:, :, 0:n], scalar1=FREQ_RATIO**n, scalar2=None, op0=ALU.mult
        )
    whole = work.tile([P, ROUNDS, HALF], F32)
    nc.vector.tensor_scalar(out=whole[:], in0=turns[:], scalar1=ROUND_MAGIC, scalar2=None, op0=ALU.add)
    minus_f = work.tile([P, ROUNDS, HALF], F32)
    nc.vector.scalar_tensor_tensor(
        out=minus_f[:], in0=whole[:], scalar=ROUND_MAGIC, in1=turns[:], op0=ALU.subtract, op1=ALU.subtract
    )
    emb = work.tile([P, ROUNDS, E], F32)
    nc.scalar.activation(out=emb[:, :, 0:HALF], in_=minus_f[:], func=ACT.Sin, scale=-2.0 * math.pi)
    nc.scalar.activation(out=minus_f[:], in_=minus_f[:], func=ACT.Abs)
    nc.scalar.activation(
        out=emb[:, :, HALF:E], in_=minus_f[:], func=ACT.Sin, scale=-2.0 * math.pi, bias=quarter_turn[:]
    )
    nc.scalar.activation(out=tables[:, :, 0, :], in_=emb[:], func=ACT.Sin, bias=quarter_turn[:])
    nc.scalar.activation(out=tables[:, :, 1, 0:HALF], in_=emb[:, :, 0:HALF], func=ACT.Sin, scale=-1.0)
    nc.scalar.activation(out=tables[:, :, 1, HALF:E], in_=emb[:, :, HALF:E], func=ACT.Sin)


def tile_rotaryembeddingtransformerlayer_pa_t_kernel(
    tc, src, Wqkv, bqkv, g1, be1, out_0, out_1, out_2
):
    nc = tc.nc
    with (
        tc.tile_pool(name="const", bufs=1) as const,
        tc.tile_pool(name="work", bufs=1) as work,
        tc.tile_pool(name="xin", bufs=3) as xin,
        tc.tile_pool(name="small", bufs=3) as small,
        tc.tile_pool(name="norm", bufs=2) as norm,
        tc.tile_pool(name="planes", bufs=1) as plane_pool,
        tc.tile_pool(name="quant", bufs=2) as quant,
        tc.tile_pool(name="mix", bufs=2) as mix,
        tc.psum_pool(name="psum_t", bufs=T_BANKS) as psum_t,
        tc.psum_pool(name="psum_acc", bufs=3) as psum_acc,
        tc.psum_pool(name="psum_tab", bufs=1) as psum_tab,
        tc.manual_schedule(),
    ):
        ident_f32 = const.tile([P, P], F32)
        ident_bf16 = const.tile([P, P], BF16)
        minus_half = const.tile([P, BATCH], F32)
        gain = const.tile([P, 2 * CHUNKS], F32)
        bias_all = const.tile([P, N_OUT], BF16)
        w_codes = const.tile([P, PASSES, N_OUT], U32, align_bytes=64)
        w_scales = const.tile([P, PASSES, N_OUT], U8, align_bytes=64)
        tables = const.tile([P, ROUNDS, 2, E], F32)
        w_rows = work.tile([P, N_OUT // P, D], BF16)
        gain_rows = work.tile([P, P], BF16)

        x_of, moments_of, rstd_of, shift_of, z_of, zT_of = {}, {}, {}, {}, {}, {}
        planes_of, grouped_of, codes_of, scales_of = {}, {}, {}, {}
        qk_of, straight_of, turned_of = {}, {}, {}

        def live(t):
            return 0 <= t < ROUNDS

        def rows(t):
            return slice(t * P, (t + 1) * P)

        def load(t):
            x_of[t] = xin.tile([P, BATCH, D], BF16, name="x")
            nc.sync.dma_start(out=x_of[t][:], in_=src[:, rows(t), :].rearrange("b p k -> p b k"))

        def statistics(t):
            x = x_of[t]
            stats = small.tile([P, BATCH, D // BN_CHUNK, 6], F32, name="stats")
            mean_var = small.tile([P, BATCH, 2], F32, name="mean_var")
            for b in range(BATCH):
                for h in range(D // BN_CHUNK):
                    nc.vector.bn_stats(out=stats[:, b, h, :], in_=x[:, b, h * BN_CHUNK : (h + 1) * BN_CHUNK])
            for b in range(BATCH):
                nc.vector.bn_aggr(out=mean_var[:, b, :], in_=stats[:, b, :, :].rearrange("p h s -> p (h s)"))
            moments_of[t] = mean_var

        def scale_and_shift(t):
            var_eps = small.tile([P, BATCH], F32, name="var_eps")
            nc.gpsimd.tensor_scalar(
                out=var_eps[:], in0=moments_of[t][:, :, 1], scalar1=1.0, scalar2=EPS, op0=ALU.mult, op1=ALU.add
            )
            minus_mean = small.tile([P, BATCH], F32, name="minus_mean")
            nc.gpsimd.tensor_scalar(
                out=minus_mean[:], in0=moments_of[t][:, :, 0], scalar1=-1.0, scalar2=0.0, op0=ALU.mult, op1=ALU.add
            )
            rstd_of[t] = small.tile([P, BATCH], F32, name="rstd")
            nc.gpsimd.tensor_tensor(out=rstd_of[t][:], in0=var_eps[:], in1=minus_half[:], op=ALU.pow)
            shift_of[t] = small.tile([P, BATCH], F32, name="shift")
            nc.gpsimd.tensor_tensor(out=shift_of[t][:], in0=minus_mean[:], in1=rstd_of[t][:], op=ALU.mult)

        def normalise_last(t):
            z_of[t] = norm.tile([P, BATCH, D], F32, name="z")
            for b in range(BATCH - NORM_ON_GPSIMD, BATCH):
                nc.gpsimd.tensor_scalar(
                    out=z_of[t][:, b, :], in0=x_of[t][:, b, :], scalar1=rstd_of[t][:, b : b + 1],
                    scalar2=shift_of[t][:, b : b + 1], op0=ALU.mult, op1=ALU.add,
                )

        def normalise(t):
            for b in range(BATCH - NORM_ON_GPSIMD):
                nc.scalar.activation(
                    out=z_of[t][:, b, :], in_=x_of[t][:, b, :], func=ACT.Identity,
                    scale=rstd_of[t][:, b : b + 1], bias=shift_of[t][:, b : b + 1],
                )

        def transpose(t, kc):
            zT_of[t, kc] = psum_t.tile([P, TOKENS], F32, name="zT")
            for b in range(BATCH):
                nc.tensor.transpose(
                    zT_of[t, kc][:, b * P : (b + 1) * P], z_of[t][:, b, kc * P : (kc + 1) * P], ident_f32[:]
                )

        def gain_out(t, kc):
            if kc == 0:
                planes_of[t] = plane_pool.tile([P, CHUNKS, TOKENS], BF16, name="planes")
            nc.scalar.activation(
                out=planes_of[t][:, kc, :], in_=zT_of[t, kc][:], func=ACT.Identity,
                scale=gain[:, kc : kc + 1], bias=gain[:, CHUNKS + kc : CHUNKS + kc + 1],
            )

        def regroup(t, c):
            if c == 0:
                grouped_of[t] = quant.tile([P, PASSES, TOKENS, PACK], BF16, name="grouped", align_bytes=64)
            nc.scalar.copy(
                out=grouped_of[t][:, c, :, :].rearrange("p (m i) j -> p m j i", i=4),
                in_=planes_of[t][:, PACK * c : PACK * (c + 1), :].rearrange("p j (m i) -> p m j i", i=4),
            )

        def quantise(t):
            codes_of[t] = quant.tile([P, PASSES, TOKENS], U32, name="codes", align_bytes=64)
            scales_of[t] = quant.tile([P, PASSES, TOKENS], U8, name="scales", align_bytes=64)
            nc.vector.quantize_mx(
                out=codes_of[t][:].rearrange("p c w -> p (c w)").bitcast(FP8X4),
                scales=scales_of[t][:].rearrange("p c w -> p (c w)"),
                in_=grouped_of[t][:].rearrange("p c w j -> p (c w j)"),
            )

        def multiply(acc, t, b, lo, hi):
            tok = slice(b * P, (b + 1) * P)
            for c in range(PASSES):
                nc.tensor.matmul_mx(
                    out=acc,
                    lhsT=codes_of[t][:, c, tok].bitcast(FP8X4), lhsT_scale=scales_of[t][:, c, tok],
                    rhs=w_codes[:, c, lo:hi].bitcast(FP8X4), rhs_scale=w_scales[:, c, lo:hi],
                    start=(c == 0), stop=(c == PASSES - 1),
                )

        def turn(engine, t, first, last, sines):
            engine.tensor_tensor(
                out=turned_of[t][:, first:last].rearrange("p b q (h i) -> p (b q) h i", h=2),
                in0=qk_of[t][:, first:last].rearrange("p b q (i h) -> p (b q) h i", h=2),
                in1=sines.rearrange("p (h i) -> p h i", h=2).unsqueeze(1).to_broadcast([P, 2 * (last - first), 2, HALF]),
                op=ALU.mult,
            )

        def project(t):
            tab_ps = psum_tab.tile([P, 2, E], F32, name="tab_ps")
            nc.tensor.matmul(
                out=tab_ps[:].rearrange("p s e -> p (s e)"), lhsT=ident_f32[:],
                rhs=tables[:, t, :, :].rearrange("p s e -> p (s e)"), start=True, stop=True,
            )
            qk_of[t] = mix.tile([P, BATCH, 2, E], F32, name="qk")
            straight_of[t] = mix.tile([P, BATCH, 2, E], F32, name="straight")
            turned_of[t] = mix.tile([P, BATCH, 2, E], F32, name="turned")
            v = mix.tile([P, BATCH, E], F32, name="v")
            for b in range(BATCH):
                acc_qk = psum_acc.tile([P, 2 * E], F32, name="acc_qk", tag="acc")
                multiply(acc_qk[:], t, b, 0, 2 * E)
                nc.vector.tensor_tensor(
                    out=qk_of[t][:, b, :, :].rearrange("p q e -> p (q e)"), in0=acc_qk[:],
                    in1=bias_all[:, 0 : 2 * E], op=ALU.add,
                )
                if b % 2 == 0:
                    acc_v = psum_acc.tile([P, 2, E], F32, name="acc_v", tag="acc")
                multiply(acc_v[:, b % 2, :], t, b, 2 * E, N_OUT)
                if b % 2 == 1:
                    pair = slice(b - 1, b + 1)
                    nc.vector.tensor_tensor(
                        out=v[:, pair, :], in0=acc_v[:],
                        in1=bias_all[:, 2 * E : N_OUT].unsqueeze(1).to_broadcast([P, 2, E]), op=ALU.add,
                    )
                    nc.vector.tensor_tensor(
                        out=straight_of[t][:, pair].rearrange("p b q e -> p (b q) e"),
                        in0=qk_of[t][:, pair].rearrange("p b q e -> p (b q) e"),
                        in1=tab_ps[:, 0, :].unsqueeze(1).to_broadcast([P, 4, E]),
                        op=ALU.mult,
                    )
            turn(nc.vector, t, BATCH - TURN_ON_VECTOR, BATCH, tab_ps[:, 1, :])
            nc.sync.dma_start(out=out_2[:, rows(t), :].rearrange("b p e -> p b e"), in_=v[:])

        def finish_mix(t):
            straight, turned = straight_of[t], turned_of[t]
            turn(nc.gpsimd, t, 0, BATCH - TURN_ON_VECTOR, tables[:, t, 1, :])
            for b in range(0, BATCH, 2):
                pair = slice(b, b + 2)
                for q, out, op in ((0, out_0, ALU.add), (1, out_1, ALU.subtract)):
                    nc.gpsimd.tensor_tensor(
                        out=straight[:, pair, q, :], in0=straight[:, pair, q, :], in1=turned[:, pair, q, :], op=op
                    )
                    nc.sync.dma_start(
                        out=out[pair, rows(t), :].rearrange("b p e -> p b e"), in_=straight[:, pair, q, :]
                    )

        def prepare_gain():
            gain_ps = psum_acc.tile([P, P], BF16, name="gain_ps", tag="acc")
            nc.tensor.transpose(gain_ps[:], gain_rows[:], ident_bf16[:])
            nc.vector.tensor_copy(out=gain[:], in_=gain_ps[:, 0 : 2 * CHUNKS])

        def prepare_weights():
            w_grouped = work.tile([P, PASSES, N_OUT, PACK], BF16, name="w_grouped", align_bytes=64)
            for c in range(PASSES):
                for pair in range(N_OUT // (2 * P)):
                    wT = psum_acc.tile([P, PACK, 2 * P], BF16, name="wT", tag="acc")
                    for j in range(PACK):
                        for h in range(2):
                            k0 = (PACK * c + j) * P
                            nc.tensor.transpose(
                                wT[:, j, h * P : (h + 1) * P], w_rows[:, 2 * pair + h, k0 : k0 + P], ident_bf16[:]
                            )
                    nc.vector.tensor_copy(
                        out=w_grouped[:, c, 2 * P * pair : 2 * P * (pair + 1), :],
                        in_=wT[:].rearrange("p j n -> p n j"),
                    )
            for c in range(PASSES):
                for lo, hi in ((0, 2 * E), (2 * E, N_OUT)):
                    nc.vector.quantize_mx(
                        out=w_codes[:, c, lo:hi].bitcast(FP8X4),
                        scales=w_scales[:, c, lo:hi],
                        in_=w_grouped[:, c, lo:hi, :].rearrange("p n j -> p (n j)"),
                    )

        load(0)
        nc.vector.memset(gain_rows[:], 0.0)
        nc.sync.dma_start(out=gain_rows[0:CHUNKS, :], in_=g1.rearrange("(c p) -> c p", p=P))
        nc.sync.dma_start(out=gain_rows[CHUNKS : 2 * CHUNKS, :], in_=be1.rearrange("(c p) -> c p", p=P))
        load(1)
        nc.sync.dma_start(out=w_rows[:], in_=Wqkv.rearrange("(r p) k -> p r k", p=P))
        nc.sync.dma_start(out=bias_all[:], in_=bqkv.partition_broadcast(P))
        load(2)
        make_identity(nc, ident_f32[:])
        make_identity(nc, ident_bf16[:])
        nc.vector.memset(minus_half[:], -0.5)
        build_position_tables(nc, work, tables)
        prepare_gain()

        for i in range(-2, ROUNDS + 1):
            if live(i + 3) and i >= 0:
                load(i + 3)
            if live(i - 1):
                quantise(i - 1)
            if live(i):
                for kc in range(CHUNKS - T_BANKS):
                    gain_out(i, kc)
                    transpose(i, kc + T_BANKS)
            if live(i + 2):
                statistics(i + 2)
            if i == 0:
                prepare_weights()
            if live(i - 1):
                project(i - 1)
            if live(i):
                for kc in range(CHUNKS - T_BANKS, CHUNKS):
                    gain_out(i, kc)
            if live(i + 1):
                normalise(i + 1)
                for kc in range(T_BANKS):
                    transpose(i + 1, kc)
            if live(i + 2):
                scale_and_shift(i + 2)
                normalise_last(i + 2)
            if live(i - 1):
                finish_mix(i - 1)
            if live(i):
                regroup(i, 0)
                regroup(i, 1)
